import numpy as np
import ml_dtypes

BF16 = ml_dtypes.bfloat16


def bf(x):
    return np.asarray(x, np.float32).astype(BF16)


def f32(x):
    return np.asarray(x, np.float32)


def f64(x):
    return np.asarray(x).astype(np.float64)


def striped(idx):
    return np.tile(idx.reshape(-1, 16).T, (8, 1))


K, S, N, T, F = 256, 1024, 512, 128, 2
OFF = 0.5


def setup_inputs():
    return {"x": bf((np.random.standard_normal((F, T, N)) + OFF) / np.sqrt(T)), "clusters": bf((np.random.standard_normal((F, T, K)) + OFF) / np.sqrt(T)), "base": f32(3.0 + 0.5 * np.random.standard_normal((K, S))), "offs": striped(np.random.permutation(S)[:N])}


def reference(x, clusters, base, offs):
    idx = offs[:16].T.reshape(-1)
    xs, cs = f64(x), f64(clusters)
    parts = []
    for f in range(F):
        x2 = (xs[f] * xs[f]).sum(axis=0)[None, :]
        c2 = (cs[f] * cs[f]).sum(axis=0)[:, None]
        xc = cs[f].T @ xs[f]
        parts.append(np.sqrt(np.maximum(x2 + c2 - 2.0 * xc, 0.0)))
    out = f64(base).copy()
    out[:, idx] = parts[0] + parts[1]
    return out

@@ -1,0 +1,86 @@
+import concourse.mybir as mybir
+
+F, T, N = 2, 128, 512
+K, S = 256, 1024
+P = 128
+BLOCKS = K // P
+PIECE = 128
+ACC_BANKS = 6
+WARM_UP_MATMULS = 16
+
+BF16, F32, U16 = mybir.dt.bfloat16, mybir.dt.float32, mybir.dt.uint16
+ALU = mybir.AluOpType
+ACT = mybir.ActivationFunctionType
+
+FLOPS = 2 * F * T * K * N
+
+
+def tile_softkmeans_kernel(tc, x, clusters, base, offs, out):
+    nc = tc.nc
+    with (
+        tc.tile_pool(name="held", bufs=1) as held,
+        tc.tile_pool(name="work", bufs=2) as work,
+        tc.psum_pool(name="psum", bufs=ACC_BANKS) as psum,
+        tc.psum_pool(name="psum_held", bufs=1) as psum_held,
+    ):
+        minus_half = held.tile([T, P], BF16, name="minus_half")
+        nc.vector.memset(minus_half[:], -0.5)
+        warm_up = psum_held.tile([P, P], F32, name="warm_up")
+        for i in range(WARM_UP_MATMULS):
+            nc.tensor.matmul(warm_up[:], minus_half[:], minus_half[:], start=True, stop=True)
+
+        c_all = held.tile([T, F, K], BF16, name="c_all")
+        nc.sync.dma_start(c_all[:], clusters.rearrange("f t k -> t f k"))
+        x_of = [held.tile([T, N], BF16, name=f"x{f}") for f in range(F)]
+        for f in range(F):
+            nc.sync.dma_start(x_of[f][:], x[f])
+        offsets = held.tile([P, N // 16], U16, name="offsets")
+        nc.sync.dma_start(offsets[:], offs)
+        window_of = [held.tile([P, S], F32, name=f"window{b}") for b in range(BLOCKS)]
+        for b in range(BLOCKS):
+            nc.sync.dma_start(window_of[b][:], base[b * P : (b + 1) * P, :])
+
+        plus_half = held.tile([T, 1], BF16, name="plus_half")
+        nc.vector.memset(plus_half[:], 0.5)
+        c_squared = held.tile([T, F, K], BF16, name="c_squared")
+        nc.vector.tensor_mul(c_squared[:], c_all[:], c_all[:])
+        x_squared_of = [held.tile([T, N], BF16, name=f"x_squared{f}") for f in range(F)]
+        for f in range(F):
+            nc.vector.tensor_mul(x_squared_of[f][:], x_of[f][:], x_of[f][:])
+
+        half_c2_psum = psum_held.tile([P, BLOCKS * F], F32, name="half_c2_psum")
+        for b in range(BLOCKS):
+            for f in range(F):
+                nc.tensor.matmul(
+                    half_c2_psum[:, b * F + f : b * F + f + 1],
+                    c_squared[:, f, b * P : (b + 1) * P],
+                    plus_half[:],
+                    start=True,
+                    stop=True,
+                )
+        half_c2 = held.tile([P, BLOCKS * F], F32, name="half_c2")
+        nc.vector.tensor_copy(half_c2[:], half_c2_psum[:])
+
+        for b in range(BLOCKS):
+            block = slice(b * P, (b + 1) * P)
+            root_of = [work.tile([P, N], F32, name=f"root{f}") for f in range(F)]
+            for f in range(F):
+                clipped = work.tile([P, N], F32, name="clipped")
+                for first in range(0, N, PIECE):
+                    piece = slice(first, first + PIECE)
+                    acc = psum.tile([P, PIECE], F32, name="acc")
+                    nc.tensor.matmul(acc[:], minus_half[:], x_squared_of[f][:, piece], start=True, stop=False)
+                    nc.tensor.matmul(acc[:], c_all[:, f, block], x_of[f][:, piece], start=False, stop=True)
+
+                    this_half_c2 = half_c2[:, b * F + f : b * F + f + 1]
+                    if b == 0:
+                        nc.vector.tensor_scalar(clipped[:, piece], acc[:], this_half_c2, 0.0, ALU.subtract, ALU.min)
+                        nc.scalar.activation(root_of[f][:, piece], clipped[:, piece], ACT.Sqrt, scale=-2.0)
+                    else:
+                        nc.scalar.activation(clipped[:, piece], acc[:], ACT.Relu, bias=this_half_c2, scale=-1.0)
+                        nc.scalar.activation(root_of[f][:, piece], clipped[:, piece], ACT.Sqrt, scale=2.0)
+
+            nc.vector.tensor_tensor(
+                window_of[b][:].indirect(offsets[:]), root_of[0][:], root_of[1][:], ALU.add
+            )
+            nc.sync.dma_start(out[block, :], window_of[b][:])

@@ -45,24 +45,19 @@ def tile_softkmeans_kernel(tc, x, clusters, base, offs, out):
         c_squared = held.tile([T, F, K], BF16, name="c_squared")
         nc.vector.tensor_mul(c_squared[:], c_all[:], c_all[:])
         x_squared_of = [held.tile([T, N], BF16, name=f"x_squared{f}") for f in range(F)]
-        for f in range(F):
-            nc.vector.tensor_mul(x_squared_of[f][:], x_of[f][:], x_of[f][:])
-
-        half_c2_psum = psum_held.tile([P, BLOCKS * F], F32, name="half_c2_psum")
-        for b in range(BLOCKS):
-            for f in range(F):
-                nc.tensor.matmul(
-                    half_c2_psum[:, b * F + f : b * F + f + 1],
-                    c_squared[:, f, b * P : (b + 1) * P],
-                    plus_half[:],
-                    start=True,
-                    stop=True,
-                )
-        half_c2 = held.tile([P, BLOCKS * F], F32, name="half_c2")
-        nc.vector.tensor_copy(half_c2[:], half_c2_psum[:])
+        for f, piece in ((0, slice(0, PIECE)), (0, slice(PIECE, N)), (1, slice(0, N))):
+            nc.vector.tensor_mul(x_squared_of[f][:, piece], x_of[f][:, piece], x_of[f][:, piece])
 
         for b in range(BLOCKS):
             block = slice(b * P, (b + 1) * P)
+
+            half_c2 = psum_held.tile([P, F], F32, name="half_c2")
+            for f in range(F):
+                nc.tensor.matmul(half_c2[:, f : f + 1], c_squared[:, f, block], plus_half[:], start=True, stop=True)
+            if b == 1:
+                half_c2_bias = held.tile([P, F], F32, name="half_c2_bias")
+                nc.scalar.copy(half_c2_bias[:], half_c2[:])
+
             root_of = [work.tile([P, N], F32, name=f"root{f}") for f in range(F)]
             for f in range(F):
                 clipped = work.tile([P, N], F32, name="clipped")
@@ -72,12 +67,11 @@ def tile_softkmeans_kernel(tc, x, clusters, base, offs, out):
                     nc.tensor.matmul(acc[:], minus_half[:], x_squared_of[f][:, piece], start=True, stop=False)
                     nc.tensor.matmul(acc[:], c_all[:, f, block], x_of[f][:, piece], start=False, stop=True)
 
-                    this_half_c2 = half_c2[:, b * F + f : b * F + f + 1]
                     if b == 0:
-                        nc.vector.tensor_scalar(clipped[:, piece], acc[:], this_half_c2, 0.0, ALU.subtract, ALU.min)
+                        nc.vector.tensor_scalar(clipped[:, piece], acc[:], half_c2[:, f : f + 1], 0.0, ALU.subtract, ALU.min)
                         nc.scalar.activation(root_of[f][:, piece], clipped[:, piece], ACT.Sqrt, scale=-2.0)
                     else:
-                        nc.scalar.activation(clipped[:, piece], acc[:], ACT.Relu, bias=this_half_c2, scale=-1.0)
+                        nc.scalar.activation(clipped[:, piece], acc[:], ACT.Relu, bias=half_c2_bias[:, f : f + 1], scale=-1.0)
                         nc.scalar.activation(root_of[f][:, piece], clipped[:, piece], ACT.Sqrt, scale=2.0)
 
             nc.vector.tensor_tensor(

@@ -5,7 +5,7 @@ K, S = 256, 1024
 P = 128
 BLOCKS = K // P
 PIECE = 128
-ACC_BANKS = 6
+ACC_BANKS = 4
 WARM_UP_MATMULS = 16
 
 BF16, F32, U16 = mybir.dt.bfloat16, mybir.dt.float32, mybir.dt.uint16
@@ -42,18 +42,23 @@ def tile_softkmeans_kernel(tc, x, clusters, base, offs, out):
 
         plus_half = held.tile([T, 1], BF16, name="plus_half")
         nc.vector.memset(plus_half[:], 0.5)
-        c_squared = held.tile([T, F, K], BF16, name="c_squared")
-        nc.vector.tensor_mul(c_squared[:], c_all[:], c_all[:])
+        table_in = held.tile([P, 1], F32, name="table_in")
+        nc.scalar.activation(table_in[:], plus_half[:], ACT.Sqrt)
+        c_squared_of = [held.tile([T, F, P], BF16, name=f"c_squared{b}") for b in range(BLOCKS)]
+        nc.vector.tensor_mul(c_squared_of[0][:], c_all[:, :, :P], c_all[:, :, :P])
+        nc.scalar.activation(c_squared_of[1][:], c_all[:, :, P:], ACT.Square)
         x_squared_of = [held.tile([T, N], BF16, name=f"x_squared{f}") for f in range(F)]
-        for f, piece in ((0, slice(0, PIECE)), (0, slice(PIECE, N)), (1, slice(0, N))):
-            nc.vector.tensor_mul(x_squared_of[f][:, piece], x_of[f][:, piece], x_of[f][:, piece])
+        for piece in (slice(0, PIECE), slice(PIECE, N)):
+            nc.vector.tensor_mul(x_squared_of[0][:, piece], x_of[0][:, piece], x_of[0][:, piece])
+        for piece in (slice(0, N // 2), slice(N // 2, N)):
+            nc.scalar.activation(x_squared_of[1][:, piece], x_of[1][:, piece], ACT.Square)
 
         for b in range(BLOCKS):
             block = slice(b * P, (b + 1) * P)
 
             half_c2 = psum_held.tile([P, F], F32, name="half_c2")
             for f in range(F):
-                nc.tensor.matmul(half_c2[:, f : f + 1], c_squared[:, f, block], plus_half[:], start=True, stop=True)
+                nc.tensor.matmul(half_c2[:, f : f + 1], c_squared_of[b][:, f, :], plus_half[:], start=True, stop=True)
             if b == 1:
                 half_c2_bias = held.tile([P, F], F32, name="half_c2_bias")
                 nc.scalar.copy(half_c2_bias[:], half_c2[:])

@@ -5,7 +5,7 @@ K, S = 256, 1024
 P = 128
 BLOCKS = K // P
 PIECE = 128
-ACC_BANKS = 4
+ACC_BANKS = 6
 WARM_UP_MATMULS = 16
 
 BF16, F32, U16 = mybir.dt.bfloat16, mybir.dt.float32, mybir.dt.uint16
@@ -29,8 +29,10 @@ def tile_softkmeans_kernel(tc, x, clusters, base, offs, out):
         for i in range(WARM_UP_MATMULS):
             nc.tensor.matmul(warm_up[:], minus_half[:], minus_half[:], start=True, stop=True)
 
-        c_all = held.tile([T, F, K], BF16, name="c_all")
-        nc.sync.dma_start(c_all[:], clusters.rearrange("f t k -> t f k"))
+        c_of = [held.tile([T, F, P], BF16, name=f"c{b}") for b in range(BLOCKS)]
+        c_by_time = clusters.rearrange("f t k -> t f k")
+        nc.sync.dma_start(c_of[0][:], c_by_time[:, :, :P])
+        nc.gpsimd.dma_start(c_of[1][:], c_by_time[:, :, P:])
         x_of = [held.tile([T, N], BF16, name=f"x{f}") for f in range(F)]
         for f in range(F):
             nc.sync.dma_start(x_of[f][:], x[f])
@@ -45,13 +47,13 @@ def tile_softkmeans_kernel(tc, x, clusters, base, offs, out):
         table_in = held.tile([P, 1], F32, name="table_in")
         nc.scalar.activation(table_in[:], plus_half[:], ACT.Sqrt)
         c_squared_of = [held.tile([T, F, P], BF16, name=f"c_squared{b}") for b in range(BLOCKS)]
-        nc.vector.tensor_mul(c_squared_of[0][:], c_all[:, :, :P], c_all[:, :, :P])
-        nc.scalar.activation(c_squared_of[1][:], c_all[:, :, P:], ACT.Square)
+        nc.vector.tensor_mul(c_squared_of[0][:], c_of[0][:], c_of[0][:])
+        nc.gpsimd.tensor_mul(c_squared_of[1][:], c_of[1][:], c_of[1][:])
         x_squared_of = [held.tile([T, N], BF16, name=f"x_squared{f}") for f in range(F)]
-        for piece in (slice(0, PIECE), slice(PIECE, N)):
-            nc.vector.tensor_mul(x_squared_of[0][:, piece], x_of[0][:, piece], x_of[0][:, piece])
-        for piece in (slice(0, N // 2), slice(N // 2, N)):
-            nc.scalar.activation(x_squared_of[1][:, piece], x_of[1][:, piece], ACT.Square)
+        for half in (slice(0, N // 2), slice(N // 2, N)):
+            nc.vector.tensor_mul(x_squared_of[0][:, half], x_of[0][:, half], x_of[0][:, half])
+        nc.vector.tensor_mul(x_squared_of[1][:, : N // 2], x_of[1][:, : N // 2], x_of[1][:, : N // 2])
+        nc.scalar.activation(x_squared_of[1][:, N // 2 :], x_of[1][:, N // 2 :], ACT.Square)
 
         for b in range(BLOCKS):
             block = slice(b * P, (b + 1) * P)
@@ -70,7 +72,7 @@ def tile_softkmeans_kernel(tc, x, clusters, base, offs, out):
                     piece = slice(first, first + PIECE)
                     acc = psum.tile([P, PIECE], F32, name="acc")
                     nc.tensor.matmul(acc[:], minus_half[:], x_squared_of[f][:, piece], start=True, stop=False)
-                    nc.tensor.matmul(acc[:], c_all[:, f, block], x_of[f][:, piece], start=False, stop=True)
+                    nc.tensor.matmul(acc[:], c_of[b][:, f, :], x_of[f][:, piece], start=False, stop=True)
 
                     if b == 0:
                         nc.vector.tensor_scalar(clipped[:, piece], acc[:], half_c2[:, f : f + 1], 0.0, ALU.subtract, ALU.min)

@@ -32,15 +32,15 @@ def tile_softkmeans_kernel(tc, x, clusters, base, offs, out):
         c_of = [held.tile([T, F, P], BF16, name=f"c{b}") for b in range(BLOCKS)]
         c_by_time = clusters.rearrange("f t k -> t f k")
         nc.sync.dma_start(c_of[0][:], c_by_time[:, :, :P])
-        nc.gpsimd.dma_start(c_of[1][:], c_by_time[:, :, P:])
         x_of = [held.tile([T, N], BF16, name=f"x{f}") for f in range(F)]
         for f in range(F):
             nc.sync.dma_start(x_of[f][:], x[f])
+        nc.sync.dma_start(c_of[1][:], c_by_time[:, :, P:])
         offsets = held.tile([P, N // 16], U16, name="offsets")
         nc.sync.dma_start(offsets[:], offs)
         window_of = [held.tile([P, S], F32, name=f"window{b}") for b in range(BLOCKS)]
-        for b in range(BLOCKS):
-            nc.sync.dma_start(window_of[b][:], base[b * P : (b + 1) * P, :])
+        nc.sync.dma_start(window_of[0][:], base[:P, :])
+        nc.gpsimd.dma_start(window_of[1][:], base[P:, :])
 
         plus_half = held.tile([T, 1], BF16, name="plus_half")
         nc.vector.memset(plus_half[:], 0.5)

import concourse.mybir as mybir

F, T, N = 2, 128, 512
K, S = 256, 1024
P = 128
BLOCKS = K // P
PIECE = 128
ACC_BANKS = 6
WARM_UP_MATMULS = 16

BF16, F32, U16 = mybir.dt.bfloat16, mybir.dt.float32, mybir.dt.uint16
ALU = mybir.AluOpType
ACT = mybir.ActivationFunctionType

FLOPS = 2 * F * T * K * N


def tile_softkmeans_kernel(tc, x, clusters, base, offs, out):
    nc = tc.nc
    with (
        tc.tile_pool(name="held", bufs=1) as held,
        tc.tile_pool(name="work", bufs=2) as work,
        tc.psum_pool(name="psum", bufs=ACC_BANKS) as psum,
        tc.psum_pool(name="psum_held", bufs=1) as psum_held,
    ):
        minus_half = held.tile([T, P], BF16, name="minus_half")
        nc.vector.memset(minus_half[:], -0.5)
        warm_up = psum_held.tile([P, P], F32, name="warm_up")
        for i in range(WARM_UP_MATMULS):
            nc.tensor.matmul(warm_up[:], minus_half[:], minus_half[:], start=True, stop=True)

        c_of = [held.tile([T, F, P], BF16, name=f"c{b}") for b in range(BLOCKS)]
        c_by_time = clusters.rearrange("f t k -> t f k")
        nc.sync.dma_start(c_of[0][:], c_by_time[:, :, :P])
        x_of = [held.tile([T, N], BF16, name=f"x{f}") for f in range(F)]
        for f in range(F):
            nc.sync.dma_start(x_of[f][:], x[f])
        nc.sync.dma_start(c_of[1][:], c_by_time[:, :, P:])
        offsets = held.tile([P, N // 16], U16, name="offsets")
        nc.sync.dma_start(offsets[:], offs)
        window_of = [held.tile([P, S], F32, name=f"window{b}") for b in range(BLOCKS)]
        nc.sync.dma_start(window_of[0][:], base[:P, :])
        nc.gpsimd.dma_start(window_of[1][:], base[P:, :])

        plus_half = held.tile([T, 1], BF16, name="plus_half")
        nc.vector.memset(plus_half[:], 0.5)
        table_in = held.tile([P, 1], F32, name="table_in")
        nc.scalar.activation(table_in[:], plus_half[:], ACT.Sqrt)
        c_squared_of = [held.tile([T, F, P], BF16, name=f"c_squared{b}") for b in range(BLOCKS)]
        nc.vector.tensor_mul(c_squared_of[0][:], c_of[0][:], c_of[0][:])
        nc.gpsimd.tensor_mul(c_squared_of[1][:], c_of[1][:], c_of[1][:])
        x_squared_of = [held.tile([T, N], BF16, name=f"x_squared{f}") for f in range(F)]
        for half in (slice(0, N // 2), slice(N // 2, N)):
            nc.vector.tensor_mul(x_squared_of[0][:, half], x_of[0][:, half], x_of[0][:, half])
        nc.vector.tensor_mul(x_squared_of[1][:, : N // 2], x_of[1][:, : N // 2], x_of[1][:, : N // 2])
        nc.scalar.activation(x_squared_of[1][:, N // 2 :], x_of[1][:, N // 2 :], ACT.Square)

        for b in range(BLOCKS):
            block = slice(b * P, (b + 1) * P)

            half_c2 = psum_held.tile([P, F], F32, name="half_c2")
            for f in range(F):
                nc.tensor.matmul(half_c2[:, f : f + 1], c_squared_of[b][:, f, :], plus_half[:], start=True, stop=True)
            if b == 1:
                half_c2_bias = held.tile([P, F], F32, name="half_c2_bias")
                nc.scalar.copy(half_c2_bias[:], half_c2[:])

            root_of = [work.tile([P, N], F32, name=f"root{f}") for f in range(F)]
            for f in range(F):
                clipped = work.tile([P, N], F32, name="clipped")
                for first in range(0, N, PIECE):
                    piece = slice(first, first + PIECE)
                    acc = psum.tile([P, PIECE], F32, name="acc")
                    nc.tensor.matmul(acc[:], minus_half[:], x_squared_of[f][:, piece], start=True, stop=False)
                    nc.tensor.matmul(acc[:], c_of[b][:, f, :], x_of[f][:, piece], start=False, stop=True)

                    if b == 0:
                        nc.vector.tensor_scalar(clipped[:, piece], acc[:], half_c2[:, f : f + 1], 0.0, ALU.subtract, ALU.min)
                        nc.scalar.activation(root_of[f][:, piece], clipped[:, piece], ACT.Sqrt, scale=-2.0)
                    else:
                        nc.scalar.activation(clipped[:, piece], acc[:], ACT.Relu, bias=half_c2_bias[:, f : f + 1], scale=-1.0)
                        nc.scalar.activation(root_of[f][:, piece], clipped[:, piece], ACT.Sqrt, scale=2.0)

            nc.vector.tensor_tensor(
                window_of[b][:].indirect(offsets[:]), root_of[0][:], root_of[1][:], ALU.add
            )
            nc.sync.dma_start(out[block, :], window_of[b][:])
